import numpy as np
import ml_dtypes


def mxq(x, axis, fmt="e4m3"):
    dtype, down = {"e4m3": (ml_dtypes.float8_e4m3fn, 7), "e5m2": (ml_dtypes.float8_e5m2, 14)}[fmt]
    v = np.moveaxis(np.asarray(x, np.float32).astype(ml_dtypes.bfloat16).astype(np.float64), axis, -1)
    blocks = v.reshape(v.shape[:-1] + (-1, 32))
    amax = np.abs(blocks).max(-1, keepdims=True)
    byte = np.maximum(np.where(amax > 0, np.frexp(amax)[1] - 1 + 127, 0) - down, 1)
    scale = np.exp2(byte - 127.0)
    codes = (blocks / scale).astype(np.float32).astype(dtype).astype(np.float64)
    return np.moveaxis((codes * scale).reshape(v.shape), -1, axis)


WIDE = False


def mx_kscale(k):
    if not WIDE:
        return np.ones(k)
    levels = np.array([18, -18])
    if k % 512:
        return np.exp2(np.random.permutation(np.resize(levels, k // 32))).repeat(32)
    a = np.empty((k // 512, 16))
    for p in range(k // 512):
        a[p, :8] = np.random.permutation(np.resize(levels, 8))
        for g in range(8):
            far = levels[np.abs(levels - a[p, g]) >= 10]
            a[p, g + 8] = far[np.random.randint(len(far))]
    return np.exp2(a.ravel()).repeat(32)


BF16 = ml_dtypes.bfloat16


def bf(x):
    return np.asarray(x, np.float32).astype(BF16)


def f64(x):
    return np.asarray(x).astype(np.float64)


N, C, H, W = 4, 512, 32, 32
T = N * H * W

REPARAM_OFFSET = 2.0 ** -18
PEDESTAL = REPARAM_OFFSET ** 2
BETA_MIN = 1e-6
BOUND_BETA = (BETA_MIN + PEDESTAL) ** 0.5
BOUND_GAMMA = PEDESTAL ** 0.5


def nn_reparam(v, bound):
    return np.square(np.maximum(v, bound)) - PEDESTAL


def denominator(x, beta, gamma):
    beta_eff = nn_reparam(beta, BOUND_BETA)
    gamma_eff = nn_reparam(gamma, BOUND_GAMMA)
    return (gamma_eff @ (x * x).reshape(N, C, H * W)).reshape(N, C, H, W) + beta_eff[None, :, None, None]


def tokens(v):
    return v.transpose(1, 0, 2, 3).reshape(C, T)


def half_power(k):
    return np.exp2(np.frexp(np.sqrt(k))[1] - 1.0)


def setup_inputs():
    ks = mx_kscale(T)
    s = half_power(ks / ks.min()).reshape(N, 1, H, W)
    v = half_power(mx_kscale(C))
    vc = v[None, :, None, None]
    amp = np.exp(0.5 * np.random.standard_normal((N, 1, H, W)))
    x0 = bf(np.random.standard_normal((N, C, H, W)) * amp)
    beta = bf(np.random.standard_normal(C))
    gamma0 = bf(np.random.standard_normal((C, C)) * 1.5 / np.sqrt(C) + 0.7 * np.eye(C))
    spread = np.exp2(np.random.randint(-6, 1, (N, 1, H, W)))
    g = bf(4.0 * np.random.standard_normal((N, C, H, W)) * spread / s ** 3 * vc)
    d = denominator(f64(x0), f64(beta), f64(gamma0))
    return {"x": bf(f64(x0) * s * vc), "beta": beta, "gamma": bf(f64(gamma0) / v[:, None]),
            "denom_sq": np.asarray(d, np.float32), "grad_out": g}


def reference(x, beta, gamma, denom_sq, grad_out):
    xt = tokens(f64(x))
    gt = tokens(f64(grad_out))
    dt = tokens(f64(denom_sq))
    gm = f64(gamma)
    gamma_eff = nn_reparam(gm, BOUND_GAMMA)
    norm = 1.0 / np.sqrt(dt)
    dd = -0.5 * gt * xt * norm / dt
    dx2 = mxq(gamma_eff, 0, "e4m3").T @ mxq(dd, 0, "e5m2")
    dx = gt * norm + 2.0 * xt * dx2
    dgamma_eff = mxq(dd, 1, "e5m2") @ mxq(xt * xt, 1, "e4m3").T
    dgamma = np.where(gm > BOUND_GAMMA, 2.0 * gm * dgamma_eff, 0.0)
    return dx.reshape(C, N, H, W).transpose(1, 0, 2, 3), dgamma

@@ -1,0 +1,335 @@
+from contextlib import ExitStack
+
+import concourse.mybir as mybir
+from concourse.masks import make_identity
+
+N_IMG, C, HW = 4, 512, 1024
+T = N_IMG * HW
+W = 512
+CHUNKS = T // W
+P = 128
+J = 4
+BOUND = 2.0**-18
+PEDESTAL = 2.0**-36
+
+FLOPS = 2 * (2 * C * C * T)
+BYTES = 2 * C * T + 2 * C * T + 4 * C * T + 2 * C * C + 4 * C * T + 4 * C * C
+
+F32 = mybir.dt.float32
+BF16 = mybir.dt.bfloat16
+U32 = mybir.dt.uint32
+U8 = mybir.dt.uint8
+E4M3 = mybir.dt.float8_e4m3fn_x4
+E5M2 = mybir.dt.float8_e5m2_x4
+ALU = mybir.AluOpType
+ACT = mybir.ActivationFunctionType
+
+
+def tile_einsumgdn_v_kernel(tc, x, beta, gamma, denom_sq, grad_out, out_0, out_1):
+    nc = tc.nc
+    XP = range(1, 7)
+    with ExitStack() as ctx:
+        keep = ctx.enter_context(tc.tile_pool(name="keep", bufs=1))
+        load = ctx.enter_context(tc.tile_pool(name="load", bufs=3))
+        work = ctx.enter_context(tc.tile_pool(name="work", bufs=2))
+        psum = ctx.enter_context(tc.psum_pool(name="psum", bufs=2))
+        accs = ctx.enter_context(tc.psum_pool(name="accs", bufs=1))
+        ctx.enter_context(tc.manual_schedule())
+
+        def chunk_view(t, k):
+            n, h = divmod(k * W, HW)
+            return t[n].rearrange("(p j) h w -> p j (h w)", j=J)[:, :, h : h + W]
+
+        xs, gs, ds, ams, n2s, dds, xqs, dts, dis, os_ = {}, {}, {}, {}, {}, {}, {}, {}, {}, {}
+        dxs = {}
+
+        warm = keep.tile([P, 1], F32, name="warm")
+        nc.vector.memset(warm[:], 1.0)
+        nc.scalar.activation(out=warm[:], in_=warm[:], func=ACT.Abs_reciprocal_sqrt)
+        ident = keep.tile([P, P], F32, name="ident")
+        make_identity(nc, ident[:])
+        ident_bf = keep.tile([P, P], BF16, name="ident_bf")
+        make_identity(nc, ident_bf[:])
+
+        gm = keep.tile([P, J, C], BF16, name="gm")
+
+        def load_chunk(k, pieces):
+            ds[k] = load.tile([P, J, W], F32, name="d")
+            gs[k] = load.tile([P, J, W], BF16, name="g")
+            xs[k] = load.tile([P, J, W], BF16, name="x", bufs=4)
+            dv, gv, xv = chunk_view(denom_sq, k), chunk_view(grad_out, k), chunk_view(x, k)
+            step = J // pieces
+            for a in range(0, J, step):
+                js = slice(a, a + step)
+                nc.sync.dma_start(out=ds[k][:, js, :], in_=dv[:, js, :])
+                nc.sync.dma_start(out=gs[k][:, js, :], in_=gv[:, js, :])
+                nc.sync.dma_start(out=xs[k][:, js, :], in_=xv[:, js, :])
+            if k == 0:
+                nc.sync.dma_start(out=gm[:], in_=gamma.rearrange("(p j) c -> p j c", j=J))
+
+        def norm(k, js=slice(0, J)):
+            v = ds[k][:, js, :]
+            nc.scalar.activation(out=v, in_=v, func=ACT.Abs_reciprocal_sqrt)
+
+        def sq(k, js=slice(0, J)):
+            if k not in n2s:
+                n2s[k] = work.tile([P, J, W], F32, name="n2")
+            nc.scalar.activation(out=n2s[k][:, js, :], in_=ds[k][:, js, :], func=ACT.Square)
+
+        def mul_a(k, js=slice(0, J)):
+            if k not in ams:
+                ams[k] = load.tile([P, J, W], F32, name="a")
+            nc.vector.tensor_tensor(out=ams[k][:, js, :], in0=gs[k][:, js, :], in1=ds[k][:, js, :], op=ALU.mult)
+
+        xps = {}
+
+        def spread_x(k):
+            for h in range(2):
+                xps[k, h] = psum.tile([P, J, 256], BF16, name="xp")
+                for b in range(2):
+                    nc.tensor.matmul(
+                        out=xps[k, h][:, 2 * b : 2 * b + 2, :],
+                        lhsT=ident_bf[:],
+                        rhs=xs[k][:, 2 * b : 2 * b + 2, 256 * h : 256 * h + 256],
+                        start=True,
+                        stop=True,
+                    )
+
+        def mul_xr(k, h):
+            v = n2s[k][:, :, 256 * h : 256 * h + 256]
+            x_in = xps[k, h][:] if k in XP else xs[k][:, :, 256 * h : 256 * h + 256]
+            nc.vector.tensor_tensor(out=v, in0=x_in, in1=v, op=ALU.mult)
+
+        def mul_xr_j(k, j):
+            v = n2s[k][:, j, :]
+            nc.vector.tensor_tensor(out=v, in0=xs[k][:, j, :], in1=v, op=ALU.mult)
+
+        def mul_dd(k, h):
+            if h == 0:
+                dds[k] = work.tile([P, J, W], BF16, name="dd")
+            w = slice(256 * h, 256 * h + 256)
+            nc.vector.scalar_tensor_tensor(
+                out=dds[k][:, :, w], in0=ams[k][:, :, w], scalar=-0.5, in1=n2s[k][:, :, w], op0=ALU.mult, op1=ALU.mult
+            )
+
+        def transposes(src):
+            banks = []
+            for b in range(2):
+                tr = psum.tile([P, 2, 2, P], F32, name="tr")
+                for jj in range(2):
+                    words = src[:, 2 * b + jj, :].bitcast(F32)
+                    for u in range(2):
+                        nc.tensor.transpose(tr[:, u, jj, :], words[:, u::2], ident[:])
+                banks.append(tr)
+            return banks
+
+        def copy_x(k, banks):
+            xqs[k] = work.tile([P, C, 4], BF16, name="xsq", align_bytes=64)
+            for b in range(2):
+                nc.scalar.activation(
+                    out=xqs[k][:, 256 * b : 256 * b + 256, :].rearrange("q c (u e) -> q c u e", u=2),
+                    in_=banks[b][:].rearrange("q u j p -> q (u j p)").bitcast(BF16).rearrange("q (u c e) -> q c u e", u=2, e=2),
+                    func=ACT.Square,
+                )
+
+        def copy_dd(k, banks):
+            dts[k] = work.tile([P, C, 4], BF16, name="ddt", align_bytes=64)
+            for b in range(2):
+                nc.scalar.copy(
+                    out=dts[k][:, 256 * b : 256 * b + 256, :].rearrange("q c t -> q (c t)").bitcast(F32).rearrange("q (c u) -> q c u", u=2),
+                    in_=banks[b][:].rearrange("q u j p -> q (j p) u"),
+                )
+
+        def interleave(k, h):
+            if h == 0:
+                dis[k] = work.tile([P, W, J], BF16, name="ddi", align_bytes=64)
+            w = slice(256 * h, 256 * h + 256)
+            nc.scalar.copy(out=dis[k][:, w, :], in_=dds[k][:, :, w].rearrange("p j w -> p w j"))
+
+        def quantise(src, name, fmt, bufs):
+            cols = src.shape[1]
+            codes = work.tile([P, cols], U32, name=name + "_codes", align_bytes=64, bufs=bufs)
+            scales = work.tile([P, cols], U8, name=name + "_scales", align_bytes=64, bufs=bufs)
+            nc.vector.quantize_mx(
+                out=codes[:].bitcast(fmt), scales=scales[:], in_=src[:].rearrange("p c t -> p (c t)")
+            )
+            return codes, scales
+
+        acc = {j: accs.tile([P, C], F32, name="acc%d" % j) for j in range(2)}
+
+        gmax = keep.tile([P, J, C], BF16, name="gmax")
+        gsq = keep.tile([P, J, C], F32, name="gsq")
+        geff = keep.tile([P, C, J], BF16, name="geff", align_bytes=64)
+        gw = keep.tile([P, J, C], BF16, name="gw")
+        g_codes = keep.tile([P, C], U32, name="g_codes", align_bytes=64)
+        g_scales = keep.tile([P, C], U8, name="g_scales", align_bytes=64)
+
+        def gamma_prep():
+            nc.vector.tensor_scalar_max(out=gmax[:], in0=gm[:], scalar1=BOUND)
+            nc.vector.tensor_tensor(out=gsq[:], in0=gmax[:], in1=gmax[:], op=ALU.mult)
+
+        def gamma_mask():
+            nc.vector.scalar_tensor_tensor(
+                out=gw[:], in0=gm[:], scalar=BOUND, in1=gm[:], op0=ALU.is_gt, op1=ALU.mult
+            )
+
+        def gamma_quantise():
+            nc.vector.tensor_scalar_sub(
+                out=geff[:].rearrange("p (m c) j -> p m c j", m=4),
+                in0=gsq[:].rearrange("p j (c m) -> p m c j", m=4),
+                scalar1=PEDESTAL,
+            )
+            nc.vector.quantize_mx(
+                out=g_codes[:].bitcast(E4M3), scales=g_scales[:], in_=geff[:].rearrange("p c j -> p (c j)")
+            )
+
+        qx, qi, qt = {}, {}, {}
+
+        def mm0(k, m):
+            dxs[k, m] = psum.tile([P, W], F32, name="dx")
+            cols = slice(P * m, P * m + P)
+            nc.tensor.matmul_mx(
+                out=dxs[k, m][:],
+                lhsT=g_codes[:, cols].bitcast(E4M3),
+                lhsT_scale=g_scales[:, cols],
+                rhs=qi[k][0][:].bitcast(E5M2),
+                rhs_scale=qi[k][1][:],
+                start=True,
+                stop=True,
+            )
+
+        def mm1(k, js):
+            for j in js:
+                cols = slice(P * j, P * j + P)
+                nc.tensor.matmul_mx(
+                    out=acc[j][:],
+                    lhsT=qt[k][0][:, cols].bitcast(E5M2),
+                    lhsT_scale=qt[k][1][:, cols],
+                    rhs=qx[k][0][:].bitcast(E4M3),
+                    rhs_scale=qx[k][1][:],
+                    start=(k == 0),
+                    stop=(k == CHUNKS - 1),
+                )
+
+        def tmp(k, m):
+            if m == 0:
+                os_[k] = work.tile([P, J, W], F32, name="o", bufs=3)
+            nc.vector.scalar_tensor_tensor(
+                out=os_[k][:, m, :], in0=dxs[k, m][:], scalar=2.0, in1=xs[k][:, m, :], op0=ALU.mult, op1=ALU.mult
+            )
+
+        def add(k, m, engine):
+            engine.tensor_tensor(out=os_[k][:, m, :], in0=os_[k][:, m, :], in1=ams[k][:, m, :], op=ALU.add)
+
+        def store(k, a, b):
+            nc.sync.dma_start(out=chunk_view(out_0, k)[:, a:b, :], in_=os_[k][:, a:b, :])
+
+        def out1(j):
+            o1 = work.tile([P, C], F32, name="o1")
+            nc.vector.scalar_tensor_tensor(
+                out=o1[:].rearrange("p (c m) -> p c m", m=4),
+                in0=acc[j][:].rearrange("p (m c) -> p c m", m=4),
+                scalar=2.0,
+                in1=gw[:, j, :].rearrange("p (c m) -> p c m", m=4),
+                op0=ALU.mult,
+                op1=ALU.mult,
+            )
+            nc.sync.dma_start(out=out_1.rearrange("(p j) c -> p j c", j=J)[:, j, :], in_=o1[:])
+
+        load_chunk(0, 4)
+        load_chunk(1, 1)
+        load_chunk(2, 1)
+
+        for j in range(J):
+            norm(0, slice(j, j + 1))
+            sq(0, slice(j, j + 1))
+        for j in range(J):
+            mul_a(0, slice(j, j + 1))
+            mul_xr_j(0, j)
+        xb = transposes(xs[0])
+        copy_x(0, xb)
+        mul_dd(0, 0)
+        interleave(0, 0)
+        mul_dd(0, 1)
+        interleave(0, 1)
+        db = transposes(dds[0])
+        copy_dd(0, db)
+        norm(1)
+        sq(1)
+        gamma_prep()
+        qx[0] = quantise(xqs[0], "qx", E4M3, CHUNKS)
+        gamma_quantise()
+        qi[0] = quantise(dis[0], "qi", E5M2, 2)
+        mm0(0, 0)
+        mm0(0, 1)
+        qt[0] = quantise(dts[0], "qt", E5M2, CHUNKS)
+        mul_a(1)
+        gamma_mask()
+
+        for k in range(CHUNKS - 1):
+            nxt = k + 1
+            if k + 3 < CHUNKS:
+                load_chunk(k + 3, 1)
+            if nxt in XP:
+                spread_x(nxt)
+            if k + 2 < CHUNKS:
+                norm(k + 2)
+            g_share = 3 if nxt in XP else 2
+            tmp(k, 0)
+            add(k, 0, nc.gpsimd)
+            mm0(k, 2)
+            tmp(k, 1)
+            add(k, 1, nc.gpsimd)
+            mm0(k, 3)
+            mm1(k, (0, 1))
+            xb = transposes(xs[nxt])
+            copy_x(nxt, xb)
+            mul_xr(nxt, 0)
+            tmp(k, 2)
+            if g_share == 3:
+                add(k, 2, nc.gpsimd)
+            tmp(k, 3)
+            mul_xr(nxt, 1)
+            if nxt == CHUNKS - 1:
+                for j in (2, 3):
+                    acc[j] = psum.tile([P, C], F32, name="xp")
+                for i in range(CHUNKS - 1):
+                    mm1(i, (2, 3))
+            mul_dd(nxt, 0)
+            interleave(nxt, 0)
+            mul_dd(nxt, 1)
+            interleave(nxt, 1)
+            db = transposes(dds[nxt])
+            copy_dd(nxt, db)
+            for m in range(g_share, J):
+                add(k, m, nc.vector)
+            store(k, 0, g_share)
+            store(k, g_share, J)
+            qx[nxt] = quantise(xqs[nxt], "qx", E4M3, CHUNKS)
+            if k + 2 < CHUNKS:
+                sq(k + 2)
+                mul_a(k + 2)
+            qi[nxt] = quantise(dis[nxt], "qi", E5M2, 2)
+            mm0(nxt, 0)
+            mm0(nxt, 1)
+            qt[nxt] = quantise(dts[nxt], "qt", E5M2, CHUNKS)
+
+        k = CHUNKS - 1
+        tmp(k, 0)
+        add(k, 0, nc.gpsimd)
+        mm0(k, 2)
+        tmp(k, 1)
+        add(k, 1, nc.gpsimd)
+        mm0(k, 3)
+        mm1(k, (0, 1, 2, 3))
+        store(k, 0, 2)
+        tmp(k, 2)
+        tmp(k, 3)
+        out1(0)
+        out1(1)
+        add(k, 2, nc.vector)
+        store(k, 2, 3)
+        add(k, 3, nc.vector)
+        store(k, 3, 4)
+        out1(2)
+        out1(3)

@@ -27,7 +27,7 @@ ACT = mybir.ActivationFunctionType
 
 def tile_einsumgdn_v_kernel(tc, x, beta, gamma, denom_sq, grad_out, out_0, out_1):
     nc = tc.nc
-    XP = range(1, 7)
+    XP = range(2, CHUNKS)
     with ExitStack() as ctx:
         keep = ctx.enter_context(tc.tile_pool(name="keep", bufs=1))
         load = ctx.enter_context(tc.tile_pool(name="load", bufs=3))
@@ -53,10 +53,10 @@ def tile_einsumgdn_v_kernel(tc, x, beta, gamma, denom_sq, grad_out, out_0, out_1
 
         gm = keep.tile([P, J, C], BF16, name="gm")
 
-        def load_chunk(k, pieces):
-            ds[k] = load.tile([P, J, W], F32, name="d")
-            gs[k] = load.tile([P, J, W], BF16, name="g")
-            xs[k] = load.tile([P, J, W], BF16, name="x", bufs=4)
+        def load_chunk(k, pieces=1):
+            ds[k] = load.tile([P, J, W], F32, name="d", bufs=2)
+            gs[k] = load.tile([P, J, W], BF16, name="g", bufs=2)
+            xs[k] = load.tile([P, J, W], BF16, name="x", bufs=5)
             dv, gv, xv = chunk_view(denom_sq, k), chunk_view(grad_out, k), chunk_view(x, k)
             step = J // pieces
             for a in range(0, J, step):
@@ -64,8 +64,6 @@ def tile_einsumgdn_v_kernel(tc, x, beta, gamma, denom_sq, grad_out, out_0, out_1
                 nc.sync.dma_start(out=ds[k][:, js, :], in_=dv[:, js, :])
                 nc.sync.dma_start(out=gs[k][:, js, :], in_=gv[:, js, :])
                 nc.sync.dma_start(out=xs[k][:, js, :], in_=xv[:, js, :])
-            if k == 0:
-                nc.sync.dma_start(out=gm[:], in_=gamma.rearrange("(p j) c -> p j c", j=J))
 
         def norm(k, js=slice(0, J)):
             v = ds[k][:, js, :]
@@ -78,7 +76,7 @@ def tile_einsumgdn_v_kernel(tc, x, beta, gamma, denom_sq, grad_out, out_0, out_1
 
         def mul_a(k, js=slice(0, J)):
             if k not in ams:
-                ams[k] = load.tile([P, J, W], F32, name="a")
+                ams[k] = load.tile([P, J, W], F32, name="a", bufs=4)
             nc.vector.tensor_tensor(out=ams[k][:, js, :], in0=gs[k][:, js, :], in1=ds[k][:, js, :], op=ALU.mult)
 
         xps = {}
@@ -104,12 +102,10 @@ def tile_einsumgdn_v_kernel(tc, x, beta, gamma, denom_sq, grad_out, out_0, out_1
             v = n2s[k][:, j, :]
             nc.vector.tensor_tensor(out=v, in0=xs[k][:, j, :], in1=v, op=ALU.mult)
 
-        def mul_dd(k, h):
-            if h == 0:
-                dds[k] = work.tile([P, J, W], BF16, name="dd")
-            w = slice(256 * h, 256 * h + 256)
+        def mul_dd(k):
+            dds[k] = work.tile([P, J, W], BF16, name="dd")
             nc.vector.scalar_tensor_tensor(
-                out=dds[k][:, :, w], in0=ams[k][:, :, w], scalar=-0.5, in1=n2s[k][:, :, w], op0=ALU.mult, op1=ALU.mult
+                out=dds[k][:], in0=ams[k][:], scalar=-0.5, in1=n2s[k][:], op0=ALU.mult, op1=ALU.mult
             )
 
         def transposes(src):
@@ -140,11 +136,12 @@ def tile_einsumgdn_v_kernel(tc, x, beta, gamma, denom_sq, grad_out, out_0, out_1
                     in_=banks[b][:].rearrange("q u j p -> q (j p) u"),
                 )
 
-        def interleave(k, h):
-            if h == 0:
-                dis[k] = work.tile([P, W, J], BF16, name="ddi", align_bytes=64)
-            w = slice(256 * h, 256 * h + 256)
-            nc.scalar.copy(out=dis[k][:, w, :], in_=dds[k][:, :, w].rearrange("p j w -> p w j"))
+        def interleave(k):
+            dis[k] = work.tile([P, W, J], BF16, name="ddi", align_bytes=64)
+            nc.scalar.copy(
+                out=dis[k][:].rearrange("p (c i) t -> p c t i", i=4),
+                in_=dds[k][:].rearrange("p t (c i) -> p c t i", i=4),
+            )
 
         def quantise(src, name, fmt, bufs):
             cols = src.shape[1]
@@ -157,28 +154,25 @@ def tile_einsumgdn_v_kernel(tc, x, beta, gamma, denom_sq, grad_out, out_0, out_1
 
         acc = {j: accs.tile([P, C], F32, name="acc%d" % j) for j in range(2)}
 
-        gmax = keep.tile([P, J, C], BF16, name="gmax")
-        gsq = keep.tile([P, J, C], F32, name="gsq")
+        gu = keep.tile([P, J, C], F32, name="gu")
         geff = keep.tile([P, C, J], BF16, name="geff", align_bytes=64)
         gw = keep.tile([P, J, C], BF16, name="gw")
         g_codes = keep.tile([P, C], U32, name="g_codes", align_bytes=64)
         g_scales = keep.tile([P, C], U8, name="g_scales", align_bytes=64)
 
         def gamma_prep():
-            nc.vector.tensor_scalar_max(out=gmax[:], in0=gm[:], scalar1=BOUND)
-            nc.vector.tensor_tensor(out=gsq[:], in0=gmax[:], in1=gmax[:], op=ALU.mult)
-
-        def gamma_mask():
-            nc.vector.scalar_tensor_tensor(
-                out=gw[:], in0=gm[:], scalar=BOUND, in1=gm[:], op0=ALU.is_gt, op1=ALU.mult
+            nc.vector.tensor_scalar(
+                out=gu[:], in0=gm[:], scalar1=BOUND, scalar2=BOUND, op0=ALU.max, op1=ALU.subtract
             )
-
-        def gamma_quantise():
-            nc.vector.tensor_scalar_sub(
-                out=geff[:].rearrange("p (m c) j -> p m c j", m=4),
-                in0=gsq[:].rearrange("p j (c m) -> p m c j", m=4),
-                scalar1=PEDESTAL,
+            nc.vector.tensor_scalar(
+                out=gw[:], in0=gm[:], scalar1=BOUND, scalar2=2.0, op0=ALU.is_gt, op1=ALU.mult
             )
+            for m in range(4):
+                u = gu[:].rearrange("p j (c m) -> p m c j", m=4)[:, m]
+                nc.vector.scalar_tensor_tensor(
+                    out=geff[:, P * m : P * m + P, :], in0=u, scalar=2 * BOUND, in1=u, op0=ALU.add, op1=ALU.mult
+                )
+            nc.vector.tensor_tensor(out=gw[:], in0=gw[:], in1=gm[:], op=ALU.mult)
             nc.vector.quantize_mx(
                 out=g_codes[:].bitcast(E4M3), scales=g_scales[:], in_=geff[:].rearrange("p c j -> p (c j)")
             )
@@ -229,90 +223,107 @@ def tile_einsumgdn_v_kernel(tc, x, beta, gamma, denom_sq, grad_out, out_0, out_1
             nc.vector.scalar_tensor_tensor(
                 out=o1[:].rearrange("p (c m) -> p c m", m=4),
                 in0=acc[j][:].rearrange("p (m c) -> p c m", m=4),
-                scalar=2.0,
+                scalar=1.0,
                 in1=gw[:, j, :].rearrange("p (c m) -> p c m", m=4),
                 op0=ALU.mult,
                 op1=ALU.mult,
             )
             nc.sync.dma_start(out=out_1.rearrange("(p j) c -> p j c", j=J)[:, j, :], in_=o1[:])
 
+        def quantise_x(k):
+            qx[k] = quantise(xqs[k], "qx", E4M3, CHUNKS)
+
+        def quantise_i(k):
+            qi[k] = quantise(dis[k], "qi", E5M2, 2)
+
+        def quantise_t(k):
+            qt[k] = quantise(dts[k], "qt", E5M2, CHUNKS)
+
         load_chunk(0, 4)
-        load_chunk(1, 1)
-        load_chunk(2, 1)
+        nc.sync.dma_start(out=gm[:], in_=gamma.rearrange("(p j) c -> p j c", j=J))
+        load_chunk(1)
 
         for j in range(J):
             norm(0, slice(j, j + 1))
             sq(0, slice(j, j + 1))
-        for j in range(J):
             mul_a(0, slice(j, j + 1))
             mul_xr_j(0, j)
-        xb = transposes(xs[0])
-        copy_x(0, xb)
-        mul_dd(0, 0)
-        interleave(0, 0)
-        mul_dd(0, 1)
-        interleave(0, 1)
-        db = transposes(dds[0])
-        copy_dd(0, db)
         norm(1)
         sq(1)
+        load_chunk(2)
+        mul_dd(0)
         gamma_prep()
-        qx[0] = quantise(xqs[0], "qx", E4M3, CHUNKS)
-        gamma_quantise()
-        qi[0] = quantise(dis[0], "qi", E5M2, 2)
-        mm0(0, 0)
-        mm0(0, 1)
-        qt[0] = quantise(dts[0], "qt", E5M2, CHUNKS)
         mul_a(1)
-        gamma_mask()
 
-        for k in range(CHUNKS - 1):
-            nxt = k + 1
-            if k + 3 < CHUNKS:
-                load_chunk(k + 3, 1)
-            if nxt in XP:
-                spread_x(nxt)
-            if k + 2 < CHUNKS:
-                norm(k + 2)
-            g_share = 3 if nxt in XP else 2
-            tmp(k, 0)
-            add(k, 0, nc.gpsimd)
-            mm0(k, 2)
-            tmp(k, 1)
-            add(k, 1, nc.gpsimd)
-            mm0(k, 3)
-            mm1(k, (0, 1))
-            xb = transposes(xs[nxt])
-            copy_x(nxt, xb)
-            mul_xr(nxt, 0)
-            tmp(k, 2)
-            if g_share == 3:
+        for k in range(-1, CHUNKS - 2):
+            if k + 4 < CHUNKS:
+                load_chunk(k + 4)
+            interleave(k + 1)
+            db = transposes(dds[k + 1])
+            copy_dd(k + 1, db)
+            if k >= 0:
+                tmp(k, 0)
+                add(k, 0, nc.gpsimd)
+                mm0(k, 2)
+                tmp(k, 1)
+                add(k, 1, nc.gpsimd)
+                mm0(k, 3)
+                mm1(k, (0, 1))
+            mul_xr(k + 2, 0)
+            if k >= 0:
+                tmp(k, 2)
                 add(k, 2, nc.gpsimd)
-            tmp(k, 3)
-            mul_xr(nxt, 1)
-            if nxt == CHUNKS - 1:
-                for j in (2, 3):
-                    acc[j] = psum.tile([P, C], F32, name="xp")
-                for i in range(CHUNKS - 1):
-                    mm1(i, (2, 3))
-            mul_dd(nxt, 0)
-            interleave(nxt, 0)
-            mul_dd(nxt, 1)
-            interleave(nxt, 1)
-            db = transposes(dds[nxt])
-            copy_dd(nxt, db)
-            for m in range(g_share, J):
-                add(k, m, nc.vector)
-            store(k, 0, g_share)
-            store(k, g_share, J)
-            qx[nxt] = quantise(xqs[nxt], "qx", E4M3, CHUNKS)
-            if k + 2 < CHUNKS:
-                sq(k + 2)
-                mul_a(k + 2)
-            qi[nxt] = quantise(dis[nxt], "qi", E5M2, 2)
-            mm0(nxt, 0)
-            mm0(nxt, 1)
-            qt[nxt] = quantise(dts[nxt], "qt", E5M2, CHUNKS)
+                tmp(k, 3)
+            mul_xr(k + 2, 1)
+            if k + 3 < CHUNKS:
+                norm(k + 3)
+            xb = transposes(xs[k + 1])
+            copy_x(k + 1, xb)
+            if k + 3 < CHUNKS:
+                sq(k + 3)
+            else:
+                xb = transposes(xs[k + 2])
+                copy_x(k + 2, xb)
+            mul_dd(k + 2)
+            if k >= 0:
+                add(k, 3, nc.vector)
+                store(k, 0, 3)
+                store(k, 3, 4)
+            quantise_i(k + 1)
+            mm0(k + 1, 0)
+            mm0(k + 1, 1)
+            quantise_t(k + 1)
+            quantise_x(k + 1)
+            if k + 3 < CHUNKS:
+                mul_a(k + 3)
+                spread_x(k + 3)
+
+        k = CHUNKS - 2
+        interleave(k + 1)
+        db = transposes(dds[k + 1])
+        copy_dd(k + 1, db)
+        tmp(k, 0)
+        add(k, 0, nc.gpsimd)
+        mm0(k, 2)
+        tmp(k, 1)
+        add(k, 1, nc.gpsimd)
+        mm0(k, 3)
+        mm1(k, (0, 1))
+        tmp(k, 2)
+        tmp(k, 3)
+        quantise_x(k + 1)
+        add(k, 2, nc.vector)
+        quantise_i(k + 1)
+        mm0(k + 1, 0)
+        mm0(k + 1, 1)
+        add(k, 3, nc.vector)
+        quantise_t(k + 1)
+        store(k, 0, 2)
+        store(k, 2, 4)
+        for j in (2, 3):
+            acc[j] = psum.tile([P, C], F32, name="xp")
+        for i in range(CHUNKS - 1):
+            mm1(i, (2, 3))
 
         k = CHUNKS - 1
         tmp(k, 0)

@@ -10,7 +10,6 @@ CHUNKS = T // W
 P = 128
 J = 4
 BOUND = 2.0**-18
-PEDESTAL = 2.0**-36
 
 FLOPS = 2 * (2 * C * C * T)
 BYTES = 2 * C * T + 2 * C * T + 4 * C * T + 2 * C * C + 4 * C * T + 4 * C * C
@@ -24,181 +23,160 @@ E5M2 = mybir.dt.float8_e5m2_x4
 ALU = mybir.AluOpType
 ACT = mybir.ActivationFunctionType
 
+PSUM_X = range(2, CHUNKS)
+FIRST, SECOND = slice(0, 2), slice(2, 4)
+ALL = slice(0, J)
+
 
 def tile_einsumgdn_v_kernel(tc, x, beta, gamma, denom_sq, grad_out, out_0, out_1):
     nc = tc.nc
-    XP = range(2, CHUNKS)
     with ExitStack() as ctx:
         keep = ctx.enter_context(tc.tile_pool(name="keep", bufs=1))
-        load = ctx.enter_context(tc.tile_pool(name="load", bufs=3))
-        work = ctx.enter_context(tc.tile_pool(name="work", bufs=2))
-        psum = ctx.enter_context(tc.psum_pool(name="psum", bufs=2))
-        accs = ctx.enter_context(tc.psum_pool(name="accs", bufs=1))
+        sb = ctx.enter_context(tc.tile_pool(name="sb", bufs=2))
+        ps = ctx.enter_context(tc.psum_pool(name="ps", bufs=2))
+        ps_acc = ctx.enter_context(tc.psum_pool(name="ps_acc", bufs=1))
         ctx.enter_context(tc.manual_schedule())
-
-        def chunk_view(t, k):
-            n, h = divmod(k * W, HW)
-            return t[n].rearrange("(p j) h w -> p j (h w)", j=J)[:, :, h : h + W]
-
-        xs, gs, ds, ams, n2s, dds, xqs, dts, dis, os_ = {}, {}, {}, {}, {}, {}, {}, {}, {}, {}
-        dxs = {}
 
         warm = keep.tile([P, 1], F32, name="warm")
         nc.vector.memset(warm[:], 1.0)
         nc.scalar.activation(out=warm[:], in_=warm[:], func=ACT.Abs_reciprocal_sqrt)
+        minus_bound = keep.tile([P, 1], F32, name="minus_bound")
+        nc.vector.memset(minus_bound[:], -BOUND)
         ident = keep.tile([P, P], F32, name="ident")
         make_identity(nc, ident[:])
         ident_bf = keep.tile([P, P], BF16, name="ident_bf")
         make_identity(nc, ident_bf[:])
-
         gm = keep.tile([P, J, C], BF16, name="gm")
+        gw = keep.tile([P, J, C], BF16, name="gw")
+        g_codes = keep.tile([P, C], U32, name="g_codes", align_bytes=64)
+        g_scales = keep.tile([P, C], U8, name="g_scales", align_bytes=64)
+        acc = [ps_acc.tile([P, C], F32, name="acc%d" % j) for j in range(J)]
 
-        def load_chunk(k, pieces=1):
-            ds[k] = load.tile([P, J, W], F32, name="d", bufs=2)
-            gs[k] = load.tile([P, J, W], BF16, name="g", bufs=2)
-            xs[k] = load.tile([P, J, W], BF16, name="x", bufs=5)
-            dv, gv, xv = chunk_view(denom_sq, k), chunk_view(grad_out, k), chunk_view(x, k)
-            step = J // pieces
-            for a in range(0, J, step):
-                js = slice(a, a + step)
-                nc.sync.dma_start(out=ds[k][:, js, :], in_=dv[:, js, :])
-                nc.sync.dma_start(out=gs[k][:, js, :], in_=gv[:, js, :])
-                nc.sync.dma_start(out=xs[k][:, js, :], in_=xv[:, js, :])
+        xs, gs, ds, ams, n2s, xps, dds, xqs, dqs, qd, qx, dxs, outs = ({} for i in range(13))
+        gamma_rows = gamma.rearrange("(p j) c -> p j c", j=J)
+        out_1_rows = out_1.rearrange("(p j) c -> p j c", j=J)
 
-        def norm(k, js=slice(0, J)):
+        def rows(t, k, js=ALL):
+            n, h = divmod(k * W, HW)
+            return t[n].rearrange("(p j) h w -> p j (h w)", j=J)[:, js, h : h + W]
+
+        def load(k, pieces=(ALL,)):
+            ds[k] = sb.tile([P, J, W], F32, name="d")
+            gs[k] = sb.tile([P, J, W], BF16, name="g")
+            xs[k] = sb.tile([P, J, W], BF16, name="x", bufs=5)
+            for js in pieces:
+                nc.sync.dma_start(out=ds[k][:, js, :], in_=rows(denom_sq, k, js))
+                nc.sync.dma_start(out=gs[k][:, js, :], in_=rows(grad_out, k, js))
+                nc.sync.dma_start(out=xs[k][:, js, :], in_=rows(x, k, js))
+
+        def norm(k, js=ALL):
             v = ds[k][:, js, :]
             nc.scalar.activation(out=v, in_=v, func=ACT.Abs_reciprocal_sqrt)
 
-        def sq(k, js=slice(0, J)):
+        def square(k, js=ALL):
             if k not in n2s:
-                n2s[k] = work.tile([P, J, W], F32, name="n2")
+                n2s[k] = sb.tile([P, J, W], F32, name="n2")
             nc.scalar.activation(out=n2s[k][:, js, :], in_=ds[k][:, js, :], func=ACT.Square)
 
-        def mul_a(k, js=slice(0, J)):
+        def mul_a(k, js=ALL):
             if k not in ams:
-                ams[k] = load.tile([P, J, W], F32, name="a", bufs=4)
+                ams[k] = sb.tile([P, J, W], F32, name="a", bufs=4)
             nc.vector.tensor_tensor(out=ams[k][:, js, :], in0=gs[k][:, js, :], in1=ds[k][:, js, :], op=ALU.mult)
 
-        xps = {}
-
-        def spread_x(k):
-            for h in range(2):
-                xps[k, h] = psum.tile([P, J, 256], BF16, name="xp")
-                for b in range(2):
-                    nc.tensor.matmul(
-                        out=xps[k, h][:, 2 * b : 2 * b + 2, :],
-                        lhsT=ident_bf[:],
-                        rhs=xs[k][:, 2 * b : 2 * b + 2, 256 * h : 256 * h + 256],
-                        start=True,
-                        stop=True,
-                    )
+        def spread_x(k, h):
+            xps[k, h] = ps.tile([P, J, W // 2], BF16, name="tr")
+            for js in (FIRST, SECOND):
+                nc.tensor.matmul(
+                    out=xps[k, h][:, js, :],
+                    lhsT=ident_bf[:],
+                    rhs=xs[k][:, js, W // 2 * h : W // 2 * (h + 1)],
+                    start=True,
+                    stop=True,
+                )
 
         def mul_xr(k, h):
-            v = n2s[k][:, :, 256 * h : 256 * h + 256]
-            x_in = xps[k, h][:] if k in XP else xs[k][:, :, 256 * h : 256 * h + 256]
-            nc.vector.tensor_tensor(out=v, in0=x_in, in1=v, op=ALU.mult)
+            v = n2s[k][:, :, W // 2 * h : W // 2 * (h + 1)]
+            nc.vector.tensor_tensor(out=v, in0=xps[k, h][:], in1=v, op=ALU.mult)
 
-        def mul_xr_j(k, j):
-            v = n2s[k][:, j, :]
-            nc.vector.tensor_tensor(out=v, in0=xs[k][:, j, :], in1=v, op=ALU.mult)
+        def mul_xr_rows(k, js):
+            v = n2s[k][:, js, :]
+            nc.vector.tensor_tensor(out=v, in0=xs[k][:, js, :], in1=v, op=ALU.mult)
 
         def mul_dd(k):
-            dds[k] = work.tile([P, J, W], BF16, name="dd")
+            dds[k] = sb.tile([P, J, W], BF16, name="dd")
             nc.vector.scalar_tensor_tensor(
                 out=dds[k][:], in0=ams[k][:], scalar=-0.5, in1=n2s[k][:], op0=ALU.mult, op1=ALU.mult
             )
 
-        def transposes(src):
-            banks = []
-            for b in range(2):
-                tr = psum.tile([P, 2, 2, P], F32, name="tr")
-                for jj in range(2):
-                    words = src[:, 2 * b + jj, :].bitcast(F32)
-                    for u in range(2):
-                        nc.tensor.transpose(tr[:, u, jj, :], words[:, u::2], ident[:])
-                banks.append(tr)
-            return banks
+        def transposes(src, half):
+            bank = ps.tile([P, 2, 2, P], F32, name="tr")
+            for jj in range(2):
+                words = src[:, 2 * half + jj, :].bitcast(F32)
+                for u in range(2):
+                    nc.tensor.transpose(bank[:, u, jj, :], words[:, u::2], ident[:])
+            return bank
 
-        def copy_x(k, banks):
-            xqs[k] = work.tile([P, C, 4], BF16, name="xsq", align_bytes=64)
-            for b in range(2):
-                nc.scalar.activation(
-                    out=xqs[k][:, 256 * b : 256 * b + 256, :].rearrange("q c (u e) -> q c u e", u=2),
-                    in_=banks[b][:].rearrange("q u j p -> q (u j p)").bitcast(BF16).rearrange("q (u c e) -> q c u e", u=2, e=2),
-                    func=ACT.Square,
-                )
-
-        def copy_dd(k, banks):
-            dts[k] = work.tile([P, C, 4], BF16, name="ddt", align_bytes=64)
-            for b in range(2):
-                nc.scalar.copy(
-                    out=dts[k][:, 256 * b : 256 * b + 256, :].rearrange("q c t -> q (c t)").bitcast(F32).rearrange("q (c u) -> q c u", u=2),
-                    in_=banks[b][:].rearrange("q u j p -> q (j p) u"),
-                )
+        def turn_x(k, half):
+            bank = transposes(xs[k], half)
+            if half == 0:
+                xqs[k] = sb.tile([P, C, 4], BF16, name="xsq", align_bytes=64)
+            pairs = bank[:].rearrange("q u j p -> q (u j p)").bitcast(BF16)
+            nc.scalar.activation(
+                out=xqs[k][:, C // 2 * half : C // 2 * (half + 1), :].rearrange("q c (u e) -> q c u e", u=2),
+                in_=pairs.rearrange("q (u c e) -> q c u e", u=2, e=2),
+                func=ACT.Square,
+            )
 
         def interleave(k):
-            dis[k] = work.tile([P, W, J], BF16, name="ddi", align_bytes=64)
+            dqs[k] = sb.tile([P, W + C, 4], BF16, name="ddq", align_bytes=64)
             nc.scalar.copy(
-                out=dis[k][:].rearrange("p (c i) t -> p c t i", i=4),
+                out=dqs[k][:, :W, :].rearrange("p (c i) t -> p c t i", i=4),
                 in_=dds[k][:].rearrange("p t (c i) -> p c t i", i=4),
             )
 
-        def quantise(src, name, fmt, bufs):
+        def turn_dd(k, half):
+            bank = transposes(dds[k], half)
+            dst = dqs[k][:, W + C // 2 * half : W + C // 2 * (half + 1), :].rearrange("q c t -> q (c t)")
+            nc.scalar.copy(
+                out=dst.bitcast(F32).rearrange("q (c u) -> q c u", u=2),
+                in_=bank[:].rearrange("q u j p -> q (j p) u"),
+            )
+
+        def quantise(src, name, fmt):
             cols = src.shape[1]
-            codes = work.tile([P, cols], U32, name=name + "_codes", align_bytes=64, bufs=bufs)
-            scales = work.tile([P, cols], U8, name=name + "_scales", align_bytes=64, bufs=bufs)
+            codes = sb.tile([P, cols], U32, name=name + "_codes", align_bytes=64, bufs=3)
+            scales = sb.tile([P, cols], U8, name=name + "_scales", align_bytes=64, bufs=3)
             nc.vector.quantize_mx(
                 out=codes[:].bitcast(fmt), scales=scales[:], in_=src[:].rearrange("p c t -> p (c t)")
             )
             return codes, scales
 
-        acc = {j: accs.tile([P, C], F32, name="acc%d" % j) for j in range(2)}
+        def quantise_dd(k):
+            qd[k] = quantise(dqs[k], "qd", E5M2)
 
-        gu = keep.tile([P, J, C], F32, name="gu")
-        geff = keep.tile([P, C, J], BF16, name="geff", align_bytes=64)
-        gw = keep.tile([P, J, C], BF16, name="gw")
-        g_codes = keep.tile([P, C], U32, name="g_codes", align_bytes=64)
-        g_scales = keep.tile([P, C], U8, name="g_scales", align_bytes=64)
-
-        def gamma_prep():
-            nc.vector.tensor_scalar(
-                out=gu[:], in0=gm[:], scalar1=BOUND, scalar2=BOUND, op0=ALU.max, op1=ALU.subtract
-            )
-            nc.vector.tensor_scalar(
-                out=gw[:], in0=gm[:], scalar1=BOUND, scalar2=2.0, op0=ALU.is_gt, op1=ALU.mult
-            )
-            for m in range(4):
-                u = gu[:].rearrange("p j (c m) -> p m c j", m=4)[:, m]
-                nc.vector.scalar_tensor_tensor(
-                    out=geff[:, P * m : P * m + P, :], in0=u, scalar=2 * BOUND, in1=u, op0=ALU.add, op1=ALU.mult
-                )
-            nc.vector.tensor_tensor(out=gw[:], in0=gw[:], in1=gm[:], op=ALU.mult)
-            nc.vector.quantize_mx(
-                out=g_codes[:].bitcast(E4M3), scales=g_scales[:], in_=geff[:].rearrange("p c j -> p (c j)")
-            )
-
-        qx, qi, qt = {}, {}, {}
+        def quantise_x(k):
+            qx[k] = quantise(xqs[k], "qx", E4M3)
 
         def mm0(k, m):
-            dxs[k, m] = psum.tile([P, W], F32, name="dx")
+            dxs[k, m] = ps.tile([P, W], F32, name="dx")
             cols = slice(P * m, P * m + P)
             nc.tensor.matmul_mx(
                 out=dxs[k, m][:],
                 lhsT=g_codes[:, cols].bitcast(E4M3),
                 lhsT_scale=g_scales[:, cols],
-                rhs=qi[k][0][:].bitcast(E5M2),
-                rhs_scale=qi[k][1][:],
+                rhs=qd[k][0][:, :W].bitcast(E5M2),
+                rhs_scale=qd[k][1][:, :W],
                 start=True,
                 stop=True,
             )
 
         def mm1(k, js):
             for j in js:
-                cols = slice(P * j, P * j + P)
+                cols = slice(W + P * j, W + P * j + P)
                 nc.tensor.matmul_mx(
                     out=acc[j][:],
-                    lhsT=qt[k][0][:, cols].bitcast(E5M2),
-                    lhsT_scale=qt[k][1][:, cols],
+                    lhsT=qd[k][0][:, cols].bitcast(E5M2),
+                    lhsT_scale=qd[k][1][:, cols],
                     rhs=qx[k][0][:].bitcast(E4M3),
                     rhs_scale=qx[k][1][:],
                     start=(k == 0),
@@ -207,124 +185,137 @@ def tile_einsumgdn_v_kernel(tc, x, beta, gamma, denom_sq, grad_out, out_0, out_1
 
         def tmp(k, m):
             if m == 0:
-                os_[k] = work.tile([P, J, W], F32, name="o", bufs=3)
+                outs[k] = sb.tile([P, J, W], F32, name="o", bufs=3)
             nc.vector.scalar_tensor_tensor(
-                out=os_[k][:, m, :], in0=dxs[k, m][:], scalar=2.0, in1=xs[k][:, m, :], op0=ALU.mult, op1=ALU.mult
+                out=outs[k][:, m, :], in0=dxs[k, m][:], scalar=2.0, in1=xs[k][:, m, :], op0=ALU.mult, op1=ALU.mult
             )
 
         def add(k, m, engine):
-            engine.tensor_tensor(out=os_[k][:, m, :], in0=os_[k][:, m, :], in1=ams[k][:, m, :], op=ALU.add)
+            engine.tensor_tensor(out=outs[k][:, m, :], in0=outs[k][:, m, :], in1=ams[k][:, m, :], op=ALU.add)
 
-        def store(k, a, b):
-            nc.sync.dma_start(out=chunk_view(out_0, k)[:, a:b, :], in_=os_[k][:, a:b, :])
+        def store(k, js=ALL):
+            nc.sync.dma_start(out=rows(out_0, k, js), in_=outs[k][:, js, :])
 
-        def out1(j):
-            o1 = work.tile([P, C], F32, name="o1")
-            nc.vector.scalar_tensor_tensor(
+        def finish_out_1(j):
+            o1 = sb.tile([P, C], F32, name="o1", bufs=4)
+            nc.vector.tensor_tensor(
                 out=o1[:].rearrange("p (c m) -> p c m", m=4),
                 in0=acc[j][:].rearrange("p (m c) -> p c m", m=4),
-                scalar=1.0,
                 in1=gw[:, j, :].rearrange("p (c m) -> p c m", m=4),
-                op0=ALU.mult,
-                op1=ALU.mult,
+                op=ALU.mult,
             )
-            nc.sync.dma_start(out=out_1.rearrange("(p j) c -> p j c", j=J)[:, j, :], in_=o1[:])
+            nc.sync.dma_start(out=out_1_rows[:, j, :], in_=o1[:])
 
-        def quantise_x(k):
-            qx[k] = quantise(xqs[k], "qx", E4M3, CHUNKS)
+        for js in (FIRST, SECOND):
+            nc.sync.dma_start(out=gm[:, js, :], in_=gamma_rows[:, js, :])
+        load(0, (FIRST, SECOND))
+        load(1)
+        gu = sb.tile([P, J, C], F32, name="o", bufs=3)
+        geff = sb.tile([P, C, J], BF16, name="xsq", align_bytes=64)
+        for js in (FIRST, SECOND):
+            nc.scalar.activation(out=gu[:, js, :], in_=gm[:, js, :], func=ACT.Relu, bias=minus_bound[:])
+            nc.vector.tensor_scalar(
+                out=gw[:, js, :], in0=gm[:, js, :], scalar1=BOUND, scalar2=2.0, op0=ALU.is_gt, op1=ALU.mult
+            )
+        nc.vector.tensor_tensor(out=gw[:], in0=gw[:], in1=gm[:], op=ALU.mult)
+        for m in range(4):
+            u = gu[:].rearrange("p j (c m) -> p m c j", m=4)[:, m]
+            nc.vector.scalar_tensor_tensor(
+                out=geff[:, P * m : P * m + P, :], in0=u, scalar=2 * BOUND, in1=u, op0=ALU.add, op1=ALU.mult
+            )
 
-        def quantise_i(k):
-            qi[k] = quantise(dis[k], "qi", E5M2, 2)
-
-        def quantise_t(k):
-            qt[k] = quantise(dts[k], "qt", E5M2, CHUNKS)
-
-        load_chunk(0, 4)
-        nc.sync.dma_start(out=gm[:], in_=gamma.rearrange("(p j) c -> p j c", j=J))
-        load_chunk(1)
-
-        for j in range(J):
-            norm(0, slice(j, j + 1))
-            sq(0, slice(j, j + 1))
-            mul_a(0, slice(j, j + 1))
-            mul_xr_j(0, j)
+        for js in (FIRST, SECOND):
+            norm(0, js)
+            square(0, js)
+            mul_a(0, js)
+            mul_xr_rows(0, js)
+        nc.vector.quantize_mx(
+            out=g_codes[:].bitcast(E4M3), scales=g_scales[:], in_=geff[:].rearrange("p c j -> p (c j)")
+        )
         norm(1)
-        sq(1)
-        load_chunk(2)
+        square(1)
+        load(2)
         mul_dd(0)
-        gamma_prep()
         mul_a(1)
 
+        x_halves = [(c, half) for c in range(CHUNKS) for half in range(2)]
         for k in range(-1, CHUNKS - 2):
+            now, third = k >= 0, k + 3 < CHUNKS
             if k + 4 < CHUNKS:
-                load_chunk(k + 4)
+                load(k + 4)
             interleave(k + 1)
-            db = transposes(dds[k + 1])
-            copy_dd(k + 1, db)
-            if k >= 0:
+            if now:
                 tmp(k, 0)
                 add(k, 0, nc.gpsimd)
                 mm0(k, 2)
                 tmp(k, 1)
                 add(k, 1, nc.gpsimd)
                 mm0(k, 3)
-                mm1(k, (0, 1))
-            mul_xr(k + 2, 0)
-            if k >= 0:
+            if k + 2 in PSUM_X:
+                mul_xr(k + 2, 0)
+            else:
+                mul_xr_rows(k + 2, ALL)
+            if now:
                 tmp(k, 2)
                 add(k, 2, nc.gpsimd)
+            turn_dd(k + 1, 0)
+            if now:
+                mm1(k, (0, 1))
+            if k + 2 in PSUM_X:
+                mul_xr(k + 2, 1)
+            if now:
                 tmp(k, 3)
-            mul_xr(k + 2, 1)
-            if k + 3 < CHUNKS:
+            if third:
                 norm(k + 3)
-            xb = transposes(xs[k + 1])
-            copy_x(k + 1, xb)
-            if k + 3 < CHUNKS:
-                sq(k + 3)
-            else:
-                xb = transposes(xs[k + 2])
-                copy_x(k + 2, xb)
+            turn_dd(k + 1, 1)
+            if now:
+                mm1(k, (2, 3))
+            for c, half in x_halves[:2]:
+                turn_x(c, half)
+            x_halves = x_halves[2:]
+            if third:
+                square(k + 3)
+            if k in (2, 4):
+                for c, half in x_halves[:1]:
+                    turn_x(c, half)
+                x_halves = x_halves[1:]
             mul_dd(k + 2)
-            if k >= 0:
+            if not third:
+                interleave(k + 2)
+                turn_dd(k + 2, 0)
+            if now:
                 add(k, 3, nc.vector)
-                store(k, 0, 3)
-                store(k, 3, 4)
-            quantise_i(k + 1)
+                store(k)
+            quantise_dd(k + 1)
             mm0(k + 1, 0)
             mm0(k + 1, 1)
-            quantise_t(k + 1)
-            quantise_x(k + 1)
-            if k + 3 < CHUNKS:
+            if third:
                 mul_a(k + 3)
-                spread_x(k + 3)
+            else:
+                turn_dd(k + 2, 1)
+            quantise_x(k + 1)
+            if k + 3 in PSUM_X:
+                spread_x(k + 3, 0)
+                spread_x(k + 3, 1)
 
         k = CHUNKS - 2
-        interleave(k + 1)
-        db = transposes(dds[k + 1])
-        copy_dd(k + 1, db)
         tmp(k, 0)
         add(k, 0, nc.gpsimd)
         mm0(k, 2)
         tmp(k, 1)
-        add(k, 1, nc.gpsimd)
         mm0(k, 3)
-        mm1(k, (0, 1))
         tmp(k, 2)
         tmp(k, 3)
+        mm1(k, range(J))
         quantise_x(k + 1)
         add(k, 2, nc.vector)
-        quantise_i(k + 1)
+        quantise_dd(k + 1)
         mm0(k + 1, 0)
         mm0(k + 1, 1)
         add(k, 3, nc.vector)
-        quantise_t(k + 1)
-        store(k, 0, 2)
-        store(k, 2, 4)
-        for j in (2, 3):
-            acc[j] = psum.tile([P, C], F32, name="xp")
-        for i in range(CHUNKS - 1):
-            mm1(i, (2, 3))
-
+        nc.gpsimd.tensor_copy(out=warm[:], in_=outs[k][:, 3, W - 1 : W])
+        add(k, 1, nc.gpsimd)
+        store(k)
         k = CHUNKS - 1
         tmp(k, 0)
         add(k, 0, nc.gpsimd)
@@ -332,15 +323,15 @@ def tile_einsumgdn_v_kernel(tc, x, beta, gamma, denom_sq, grad_out, out_0, out_1
         tmp(k, 1)
         add(k, 1, nc.gpsimd)
         mm0(k, 3)
-        mm1(k, (0, 1, 2, 3))
-        store(k, 0, 2)
         tmp(k, 2)
         tmp(k, 3)
-        out1(0)
-        out1(1)
-        add(k, 2, nc.vector)
-        store(k, 2, 3)
+        store(k, FIRST)
+        mm1(k, range(J))
+        add(k, 2, nc.gpsimd)
+        finish_out_1(0)
+        finish_out_1(1)
+        finish_out_1(2)
+        finish_out_1(3)
+        store(k, slice(2, 3))
         add(k, 3, nc.vector)
-        store(k, 3, 4)
-        out1(2)
-        out1(3)
+        store(k, slice(3, 4))

@@ -108,16 +108,16 @@ def tile_einsumgdn_v_kernel(tc, x, beta, gamma, denom_sq, grad_out, out_0, out_1
                 out=dds[k][:], in0=ams[k][:], scalar=-0.5, in1=n2s[k][:], op0=ALU.mult, op1=ALU.mult
             )
 
-        def transposes(src, half):
-            bank = ps.tile([P, 2, 2, P], F32, name="tr")
+        def transposes(src, half, tag="tr"):
+            bank = ps.tile([P, 2, 2, P], F32, name=tag)
             for jj in range(2):
                 words = src[:, 2 * half + jj, :].bitcast(F32)
                 for u in range(2):
                     nc.tensor.transpose(bank[:, u, jj, :], words[:, u::2], ident[:])
             return bank
 
-        def turn_x(k, half):
-            bank = transposes(xs[k], half)
+        def turn_x(k, half, tag="tr"):
+            bank = transposes(xs[k], half, tag)
             if half == 0:
                 xqs[k] = sb.tile([P, C, 4], BF16, name="xsq", align_bytes=64)
             pairs = bank[:].rearrange("q u j p -> q (u j p)").bitcast(BF16)
@@ -190,8 +190,8 @@ def tile_einsumgdn_v_kernel(tc, x, beta, gamma, denom_sq, grad_out, out_0, out_1
                 out=outs[k][:, m, :], in0=dxs[k, m][:], scalar=2.0, in1=xs[k][:, m, :], op0=ALU.mult, op1=ALU.mult
             )
 
-        def add(k, m, engine):
-            engine.tensor_tensor(out=outs[k][:, m, :], in0=outs[k][:, m, :], in1=ams[k][:, m, :], op=ALU.add)
+        def add(k, m, engine, w=slice(0, W)):
+            engine.tensor_tensor(out=outs[k][:, m, w], in0=outs[k][:, m, w], in1=ams[k][:, m, w], op=ALU.add)
 
         def store(k, js=ALL):
             nc.sync.dma_start(out=rows(out_0, k, js), in_=outs[k][:, js, :])
@@ -270,19 +270,18 @@ def tile_einsumgdn_v_kernel(tc, x, beta, gamma, denom_sq, grad_out, out_0, out_1
             turn_dd(k + 1, 1)
             if now:
                 mm1(k, (2, 3))
+            if k in (1, 3):
+                for c, half in x_halves[:1]:
+                    turn_x(c, half, "dx")
+                x_halves = x_halves[1:]
             for c, half in x_halves[:2]:
                 turn_x(c, half)
             x_halves = x_halves[2:]
             if third:
                 square(k + 3)
-            if k in (2, 4):
-                for c, half in x_halves[:1]:
-                    turn_x(c, half)
-                x_halves = x_halves[1:]
             mul_dd(k + 2)
             if not third:
                 interleave(k + 2)
-                turn_dd(k + 2, 0)
             if now:
                 add(k, 3, nc.vector)
                 store(k)
@@ -292,7 +291,7 @@ def tile_einsumgdn_v_kernel(tc, x, beta, gamma, denom_sq, grad_out, out_0, out_1
             if third:
                 mul_a(k + 3)
             else:
-                turn_dd(k + 2, 1)
+                turn_dd(k + 2, 0)
             quantise_x(k + 1)
             if k + 3 in PSUM_X:
                 spread_x(k + 3, 0)
@@ -304,34 +303,41 @@ def tile_einsumgdn_v_kernel(tc, x, beta, gamma, denom_sq, grad_out, out_0, out_1
         mm0(k, 2)
         tmp(k, 1)
         mm0(k, 3)
+        turn_dd(k + 1, 1)
         tmp(k, 2)
         tmp(k, 3)
         mm1(k, range(J))
         quantise_x(k + 1)
+        store(k, slice(0, 1))
         add(k, 2, nc.vector)
+        store(k, slice(2, 3))
         quantise_dd(k + 1)
         mm0(k + 1, 0)
         mm0(k + 1, 1)
         add(k, 3, nc.vector)
+        store(k, slice(3, 4))
         nc.gpsimd.tensor_copy(out=warm[:], in_=outs[k][:, 3, W - 1 : W])
         add(k, 1, nc.gpsimd)
-        store(k)
+        store(k, slice(1, 2))
         k = CHUNKS - 1
+        mm1(k, (0, 1))
         tmp(k, 0)
         add(k, 0, nc.gpsimd)
         mm0(k, 2)
         tmp(k, 1)
         add(k, 1, nc.gpsimd)
         mm0(k, 3)
-        tmp(k, 2)
-        tmp(k, 3)
-        store(k, FIRST)
-        mm1(k, range(J))
-        add(k, 2, nc.gpsimd)
+        mm1(k, (2, 3))
         finish_out_1(0)
+        tmp(k, 2)
+        add(k, 2, nc.gpsimd)
         finish_out_1(1)
+        store(k, slice(0, 1))
+        tmp(k, 3)
         finish_out_1(2)
+        store(k, slice(1, 2))
         finish_out_1(3)
         store(k, slice(2, 3))
-        add(k, 3, nc.vector)
-        store(k, slice(3, 4))
+        for w in (slice(0, W // 2), slice(W // 2, W)):
+            add(k, 3, nc.vector, w)
+            nc.sync.dma_start(out=rows(out_0, k, slice(3, 4))[:, :, w], in_=outs[k][:, 3:4, w])

@@ -257,7 +257,7 @@ def tile_einsumgdn_v_kernel(tc, x, beta, gamma, denom_sq, grad_out, out_0, out_1
                 mul_xr_rows(k + 2, ALL)
             if now:
                 tmp(k, 2)
-                add(k, 2, nc.gpsimd)
+                add(k, 2, nc.gpsimd, slice(0, 320))
             turn_dd(k + 1, 0)
             if now:
                 mm1(k, (0, 1))
@@ -283,7 +283,12 @@ def tile_einsumgdn_v_kernel(tc, x, beta, gamma, denom_sq, grad_out, out_0, out_1
             if not third:
                 interleave(k + 2)
             if now:
-                add(k, 3, nc.vector)
+                nc.vector.tensor_tensor(
+                    out=outs[k][:].rearrange("p j w -> p (j w)")[:, 2 * W + 320 :],
+                    in0=outs[k][:].rearrange("p j w -> p (j w)")[:, 2 * W + 320 :],
+                    in1=ams[k][:].rearrange("p j w -> p (j w)")[:, 2 * W + 320 :],
+                    op=ALU.add,
+                )
                 store(k)
             quantise_dd(k + 1)
             mm0(k + 1, 0)
@@ -330,13 +335,13 @@ def tile_einsumgdn_v_kernel(tc, x, beta, gamma, denom_sq, grad_out, out_0, out_1
         mm1(k, (2, 3))
         finish_out_1(0)
         tmp(k, 2)
-        add(k, 2, nc.gpsimd)
         finish_out_1(1)
         store(k, slice(0, 1))
         tmp(k, 3)
         finish_out_1(2)
         store(k, slice(1, 2))
         finish_out_1(3)
+        add(k, 2, nc.vector)
         store(k, slice(2, 3))
         for w in (slice(0, W // 2), slice(W // 2, W)):
             add(k, 3, nc.vector, w)

from contextlib import ExitStack

import concourse.mybir as mybir
from concourse.masks import make_identity

N_IMG, C, HW = 4, 512, 1024
T = N_IMG * HW
W = 512
CHUNKS = T // W
P = 128
J = 4
BOUND = 2.0**-18

FLOPS = 2 * (2 * C * C * T)
BYTES = 2 * C * T + 2 * C * T + 4 * C * T + 2 * C * C + 4 * C * T + 4 * C * C

F32 = mybir.dt.float32
BF16 = mybir.dt.bfloat16
U32 = mybir.dt.uint32
U8 = mybir.dt.uint8
E4M3 = mybir.dt.float8_e4m3fn_x4
E5M2 = mybir.dt.float8_e5m2_x4
ALU = mybir.AluOpType
ACT = mybir.ActivationFunctionType

PSUM_X = range(2, CHUNKS)
FIRST, SECOND = slice(0, 2), slice(2, 4)
ALL = slice(0, J)


def tile_einsumgdn_v_kernel(tc, x, beta, gamma, denom_sq, grad_out, out_0, out_1):
    nc = tc.nc
    with ExitStack() as ctx:
        keep = ctx.enter_context(tc.tile_pool(name="keep", bufs=1))
        sb = ctx.enter_context(tc.tile_pool(name="sb", bufs=2))
        ps = ctx.enter_context(tc.psum_pool(name="ps", bufs=2))
        ps_acc = ctx.enter_context(tc.psum_pool(name="ps_acc", bufs=1))
        ctx.enter_context(tc.manual_schedule())

        warm = keep.tile([P, 1], F32, name="warm")
        nc.vector.memset(warm[:], 1.0)
        nc.scalar.activation(out=warm[:], in_=warm[:], func=ACT.Abs_reciprocal_sqrt)
        minus_bound = keep.tile([P, 1], F32, name="minus_bound")
        nc.vector.memset(minus_bound[:], -BOUND)
        ident = keep.tile([P, P], F32, name="ident")
        make_identity(nc, ident[:])
        ident_bf = keep.tile([P, P], BF16, name="ident_bf")
        make_identity(nc, ident_bf[:])
        gm = keep.tile([P, J, C], BF16, name="gm")
        gw = keep.tile([P, J, C], BF16, name="gw")
        g_codes = keep.tile([P, C], U32, name="g_codes", align_bytes=64)
        g_scales = keep.tile([P, C], U8, name="g_scales", align_bytes=64)
        acc = [ps_acc.tile([P, C], F32, name="acc%d" % j) for j in range(J)]

        xs, gs, ds, ams, n2s, xps, dds, xqs, dqs, qd, qx, dxs, outs = ({} for i in range(13))
        gamma_rows = gamma.rearrange("(p j) c -> p j c", j=J)
        out_1_rows = out_1.rearrange("(p j) c -> p j c", j=J)

        def rows(t, k, js=ALL):
            n, h = divmod(k * W, HW)
            return t[n].rearrange("(p j) h w -> p j (h w)", j=J)[:, js, h : h + W]

        def load(k, pieces=(ALL,)):
            ds[k] = sb.tile([P, J, W], F32, name="d")
            gs[k] = sb.tile([P, J, W], BF16, name="g")
            xs[k] = sb.tile([P, J, W], BF16, name="x", bufs=5)
            for js in pieces:
                nc.sync.dma_start(out=ds[k][:, js, :], in_=rows(denom_sq, k, js))
                nc.sync.dma_start(out=gs[k][:, js, :], in_=rows(grad_out, k, js))
                nc.sync.dma_start(out=xs[k][:, js, :], in_=rows(x, k, js))

        def norm(k, js=ALL):
            v = ds[k][:, js, :]
            nc.scalar.activation(out=v, in_=v, func=ACT.Abs_reciprocal_sqrt)

        def square(k, js=ALL):
            if k not in n2s:
                n2s[k] = sb.tile([P, J, W], F32, name="n2")
            nc.scalar.activation(out=n2s[k][:, js, :], in_=ds[k][:, js, :], func=ACT.Square)

        def mul_a(k, js=ALL):
            if k not in ams:
                ams[k] = sb.tile([P, J, W], F32, name="a", bufs=4)
            nc.vector.tensor_tensor(out=ams[k][:, js, :], in0=gs[k][:, js, :], in1=ds[k][:, js, :], op=ALU.mult)

        def spread_x(k, h):
            xps[k, h] = ps.tile([P, J, W // 2], BF16, name="tr")
            for js in (FIRST, SECOND):
                nc.tensor.matmul(
                    out=xps[k, h][:, js, :],
                    lhsT=ident_bf[:],
                    rhs=xs[k][:, js, W // 2 * h : W // 2 * (h + 1)],
                    start=True,
                    stop=True,
                )

        def mul_xr(k, h):
            v = n2s[k][:, :, W // 2 * h : W // 2 * (h + 1)]
            nc.vector.tensor_tensor(out=v, in0=xps[k, h][:], in1=v, op=ALU.mult)

        def mul_xr_rows(k, js):
            v = n2s[k][:, js, :]
            nc.vector.tensor_tensor(out=v, in0=xs[k][:, js, :], in1=v, op=ALU.mult)

        def mul_dd(k):
            dds[k] = sb.tile([P, J, W], BF16, name="dd")
            nc.vector.scalar_tensor_tensor(
                out=dds[k][:], in0=ams[k][:], scalar=-0.5, in1=n2s[k][:], op0=ALU.mult, op1=ALU.mult
            )

        def transposes(src, half, tag="tr"):
            bank = ps.tile([P, 2, 2, P], F32, name=tag)
            for jj in range(2):
                words = src[:, 2 * half + jj, :].bitcast(F32)
                for u in range(2):
                    nc.tensor.transpose(bank[:, u, jj, :], words[:, u::2], ident[:])
            return bank

        def turn_x(k, half, tag="tr"):
            bank = transposes(xs[k], half, tag)
            if half == 0:
                xqs[k] = sb.tile([P, C, 4], BF16, name="xsq", align_bytes=64)
            pairs = bank[:].rearrange("q u j p -> q (u j p)").bitcast(BF16)
            nc.scalar.activation(
                out=xqs[k][:, C // 2 * half : C // 2 * (half + 1), :].rearrange("q c (u e) -> q c u e", u=2),
                in_=pairs.rearrange("q (u c e) -> q c u e", u=2, e=2),
                func=ACT.Square,
            )

        def interleave(k):
            dqs[k] = sb.tile([P, W + C, 4], BF16, name="ddq", align_bytes=64)
            nc.scalar.copy(
                out=dqs[k][:, :W, :].rearrange("p (c i) t -> p c t i", i=4),
                in_=dds[k][:].rearrange("p t (c i) -> p c t i", i=4),
            )

        def turn_dd(k, half):
            bank = transposes(dds[k], half)
            dst = dqs[k][:, W + C // 2 * half : W + C // 2 * (half + 1), :].rearrange("q c t -> q (c t)")
            nc.scalar.copy(
                out=dst.bitcast(F32).rearrange("q (c u) -> q c u", u=2),
                in_=bank[:].rearrange("q u j p -> q (j p) u"),
            )

        def quantise(src, name, fmt):
            cols = src.shape[1]
            codes = sb.tile([P, cols], U32, name=name + "_codes", align_bytes=64, bufs=3)
            scales = sb.tile([P, cols], U8, name=name + "_scales", align_bytes=64, bufs=3)
            nc.vector.quantize_mx(
                out=codes[:].bitcast(fmt), scales=scales[:], in_=src[:].rearrange("p c t -> p (c t)")
            )
            return codes, scales

        def quantise_dd(k):
            qd[k] = quantise(dqs[k], "qd", E5M2)

        def quantise_x(k):
            qx[k] = quantise(xqs[k], "qx", E4M3)

        def mm0(k, m):
            dxs[k, m] = ps.tile([P, W], F32, name="dx")
            cols = slice(P * m, P * m + P)
            nc.tensor.matmul_mx(
                out=dxs[k, m][:],
                lhsT=g_codes[:, cols].bitcast(E4M3),
                lhsT_scale=g_scales[:, cols],
                rhs=qd[k][0][:, :W].bitcast(E5M2),
                rhs_scale=qd[k][1][:, :W],
                start=True,
                stop=True,
            )

        def mm1(k, js):
            for j in js:
                cols = slice(W + P * j, W + P * j + P)
                nc.tensor.matmul_mx(
                    out=acc[j][:],
                    lhsT=qd[k][0][:, cols].bitcast(E5M2),
                    lhsT_scale=qd[k][1][:, cols],
                    rhs=qx[k][0][:].bitcast(E4M3),
                    rhs_scale=qx[k][1][:],
                    start=(k == 0),
                    stop=(k == CHUNKS - 1),
                )

        def tmp(k, m):
            if m == 0:
                outs[k] = sb.tile([P, J, W], F32, name="o", bufs=3)
            nc.vector.scalar_tensor_tensor(
                out=outs[k][:, m, :], in0=dxs[k, m][:], scalar=2.0, in1=xs[k][:, m, :], op0=ALU.mult, op1=ALU.mult
            )

        def add(k, m, engine, w=slice(0, W)):
            engine.tensor_tensor(out=outs[k][:, m, w], in0=outs[k][:, m, w], in1=ams[k][:, m, w], op=ALU.add)

        def store(k, js=ALL):
            nc.sync.dma_start(out=rows(out_0, k, js), in_=outs[k][:, js, :])

        def finish_out_1(j):
            o1 = sb.tile([P, C], F32, name="o1", bufs=4)
            nc.vector.tensor_tensor(
                out=o1[:].rearrange("p (c m) -> p c m", m=4),
                in0=acc[j][:].rearrange("p (m c) -> p c m", m=4),
                in1=gw[:, j, :].rearrange("p (c m) -> p c m", m=4),
                op=ALU.mult,
            )
            nc.sync.dma_start(out=out_1_rows[:, j, :], in_=o1[:])

        for js in (FIRST, SECOND):
            nc.sync.dma_start(out=gm[:, js, :], in_=gamma_rows[:, js, :])
        load(0, (FIRST, SECOND))
        load(1)
        gu = sb.tile([P, J, C], F32, name="o", bufs=3)
        geff = sb.tile([P, C, J], BF16, name="xsq", align_bytes=64)
        for js in (FIRST, SECOND):
            nc.scalar.activation(out=gu[:, js, :], in_=gm[:, js, :], func=ACT.Relu, bias=minus_bound[:])
            nc.vector.tensor_scalar(
                out=gw[:, js, :], in0=gm[:, js, :], scalar1=BOUND, scalar2=2.0, op0=ALU.is_gt, op1=ALU.mult
            )
        nc.vector.tensor_tensor(out=gw[:], in0=gw[:], in1=gm[:], op=ALU.mult)
        for m in range(4):
            u = gu[:].rearrange("p j (c m) -> p m c j", m=4)[:, m]
            nc.vector.scalar_tensor_tensor(
                out=geff[:, P * m : P * m + P, :], in0=u, scalar=2 * BOUND, in1=u, op0=ALU.add, op1=ALU.mult
            )

        for js in (FIRST, SECOND):
            norm(0, js)
            square(0, js)
            mul_a(0, js)
            mul_xr_rows(0, js)
        nc.vector.quantize_mx(
            out=g_codes[:].bitcast(E4M3), scales=g_scales[:], in_=geff[:].rearrange("p c j -> p (c j)")
        )
        norm(1)
        square(1)
        load(2)
        mul_dd(0)
        mul_a(1)

        x_halves = [(c, half) for c in range(CHUNKS) for half in range(2)]
        for k in range(-1, CHUNKS - 2):
            now, third = k >= 0, k + 3 < CHUNKS
            if k + 4 < CHUNKS:
                load(k + 4)
            interleave(k + 1)
            if now:
                tmp(k, 0)
                add(k, 0, nc.gpsimd)
                mm0(k, 2)
                tmp(k, 1)
                add(k, 1, nc.gpsimd)
                mm0(k, 3)
            if k + 2 in PSUM_X:
                mul_xr(k + 2, 0)
            else:
                mul_xr_rows(k + 2, ALL)
            if now:
                tmp(k, 2)
                add(k, 2, nc.gpsimd, slice(0, 320))
            turn_dd(k + 1, 0)
            if now:
                mm1(k, (0, 1))
            if k + 2 in PSUM_X:
                mul_xr(k + 2, 1)
            if now:
                tmp(k, 3)
            if third:
                norm(k + 3)
            turn_dd(k + 1, 1)
            if now:
                mm1(k, (2, 3))
            if k in (1, 3):
                for c, half in x_halves[:1]:
                    turn_x(c, half, "dx")
                x_halves = x_halves[1:]
            for c, half in x_halves[:2]:
                turn_x(c, half)
            x_halves = x_halves[2:]
            if third:
                square(k + 3)
            mul_dd(k + 2)
            if not third:
                interleave(k + 2)
            if now:
                nc.vector.tensor_tensor(
                    out=outs[k][:].rearrange("p j w -> p (j w)")[:, 2 * W + 320 :],
                    in0=outs[k][:].rearrange("p j w -> p (j w)")[:, 2 * W + 320 :],
                    in1=ams[k][:].rearrange("p j w -> p (j w)")[:, 2 * W + 320 :],
                    op=ALU.add,
                )
                store(k)
            quantise_dd(k + 1)
            mm0(k + 1, 0)
            mm0(k + 1, 1)
            if third:
                mul_a(k + 3)
            else:
                turn_dd(k + 2, 0)
            quantise_x(k + 1)
            if k + 3 in PSUM_X:
                spread_x(k + 3, 0)
                spread_x(k + 3, 1)

        k = CHUNKS - 2
        tmp(k, 0)
        add(k, 0, nc.gpsimd)
        mm0(k, 2)
        tmp(k, 1)
        mm0(k, 3)
        turn_dd(k + 1, 1)
        tmp(k, 2)
        tmp(k, 3)
        mm1(k, range(J))
        quantise_x(k + 1)
        store(k, slice(0, 1))
        add(k, 2, nc.vector)
        store(k, slice(2, 3))
        quantise_dd(k + 1)
        mm0(k + 1, 0)
        mm0(k + 1, 1)
        add(k, 3, nc.vector)
        store(k, slice(3, 4))
        nc.gpsimd.tensor_copy(out=warm[:], in_=outs[k][:, 3, W - 1 : W])
        add(k, 1, nc.gpsimd)
        store(k, slice(1, 2))
        k = CHUNKS - 1
        mm1(k, (0, 1))
        tmp(k, 0)
        add(k, 0, nc.gpsimd)
        mm0(k, 2)
        tmp(k, 1)
        add(k, 1, nc.gpsimd)
        mm0(k, 3)
        mm1(k, (2, 3))
        finish_out_1(0)
        tmp(k, 2)
        finish_out_1(1)
        store(k, slice(0, 1))
        tmp(k, 3)
        finish_out_1(2)
        store(k, slice(1, 2))
        finish_out_1(3)
        add(k, 2, nc.vector)
        store(k, slice(2, 3))
        for w in (slice(0, W // 2), slice(W // 2, W)):
            add(k, 3, nc.vector, w)
            nc.sync.dma_start(out=rows(out_0, k, slice(3, 4))[:, :, w], in_=outs[k][:, 3:4, w])
